import numpy as np
import ml_dtypes


def mxq(x, axis, fmt="e4m3"):
    dtype, down = {"e4m3": (ml_dtypes.float8_e4m3fn, 7), "e5m2": (ml_dtypes.float8_e5m2, 14)}[fmt]
    v = np.moveaxis(np.asarray(x, np.float32).astype(ml_dtypes.bfloat16).astype(np.float64), axis, -1)
    blocks = v.reshape(v.shape[:-1] + (-1, 32))
    amax = np.abs(blocks).max(-1, keepdims=True)
    byte = np.maximum(np.where(amax > 0, np.frexp(amax)[1] - 1 + 127, 0) - down, 1)
    scale = np.exp2(byte - 127.0)
    codes = (blocks / scale).astype(np.float32).astype(dtype).astype(np.float64)
    return np.moveaxis((codes * scale).reshape(v.shape), -1, axis)


WIDE = False


def mx_kscale(k):
    if not WIDE:
        return np.ones(k)
    levels = np.array([10, -10, 5, -5, 0])
    if k % 512:
        return np.exp2(np.random.permutation(np.resize(levels, k // 32))).repeat(32)
    a = np.empty((k // 512, 16))
    for p in range(k // 512):
        a[p, :8] = np.random.permutation(np.resize(levels, 8))
        for g in range(8):
            far = levels[np.abs(levels - a[p, g]) >= 10]
            a[p, g + 8] = far[np.random.randint(len(far))]
    return np.exp2(a.ravel()).repeat(32)


BF16 = ml_dtypes.bfloat16


def bf(x):
    return np.asarray(x, np.float32).astype(BF16)


def f64(x):
    return np.asarray(x).astype(np.float64)


B, I, H, G = 8192, 256, 256, 4
K = I + H


def sigmoid(v):
    return 1.0 / (1.0 + np.exp(-v))


def hardtanh(v):
    return np.clip(v, -1.0, 1.0)


def setup_inputs():
    s = mx_kscale(K)
    return {"x": bf(np.random.standard_normal((B, I)) * s[:I]),
            "state": bf(np.random.standard_normal((B, H)) * s[I:]),
            "cell": bf(np.random.standard_normal((B, H))),
            "W_in": bf(np.random.standard_normal((G, H, I)) / np.sqrt(K) / s[:I]),
            "W_h": bf(np.random.standard_normal((G, H, H)) / np.sqrt(K) / s[I:])}


def reference(x, state, cell, W_in, W_h):
    z = np.concatenate([f64(x), f64(state)], axis=1)
    W = np.concatenate([f64(W_in), f64(W_h)], axis=2)
    g = mxq(z, 1, "e4m3") @ mxq(W, 2, "e4m3").reshape(G * H, K).T
    g = g.reshape(B, G, H).transpose(1, 0, 2)
    f = sigmoid(g[0])
    i = sigmoid(g[1])
    o = sigmoid(g[2])
    u = hardtanh(g[3])
    new_cell = f * f64(cell) + i * u
    new_state = o * hardtanh(new_cell)
    return (new_state, new_cell)

@@ -1,0 +1,303 @@
+from contextlib import ExitStack
+
+import concourse.mybir as mybir
+from concourse.masks import make_identity
+
+F32 = mybir.dt.float32
+BF16 = mybir.dt.bfloat16
+U32 = mybir.dt.uint32
+U8 = mybir.dt.uint8
+FP8X4 = mybir.dt.float8_e4m3fn_x4
+ALU = mybir.AluOpType
+ACTF = mybir.ActivationFunctionType
+
+P = 128
+B, I, H, G = 8192, 256, 256, 4
+NT = B // P
+NP = NT // 2
+FLOPS = 2 * B * (I + H) * G * H
+
+MANUAL = False
+LEAD_T = 6
+LEAD_S = 2
+MARGIN = 8
+RR_FROM = 6
+RR_EVERY = 3
+D_UNTIL = 4
+
+GROUPS = [(k, 1) for k in range(4)] + [(k, 2) for k in range(4, NP - 2, 2)] + [(NP - 2, 1), (NP - 1, 1)]
+NG = len(GROUPS)
+XCH = [(0, 4), (4, 4)] + [(t, 8) for t in range(8, NT, 8)]
+FG, IG, OG, UG = 0, 1, 2, 3
+TAGS = ["F", "I", "O", "U"]
+
+
+def chunk_of(t):
+    for ci, (t0, n) in enumerate(XCH):
+        if t0 <= t < t0 + n:
+            return ci, t - t0
+    raise ValueError("tile outside the table")
+
+
+def group_of(k):
+    for g, (k0, n) in enumerate(GROUPS):
+        if k0 <= k < k0 + n:
+            return g, k - k0
+    raise ValueError("pair outside the table")
+
+
+def tile_lstmhardcell_t_kernel(tc, x, state, cell, W_in, W_h, out_0, out_1):
+    nc = tc.nc
+    with ExitStack() as ctx:
+        const = ctx.enter_context(tc.tile_pool(name="const", bufs=1))
+        inp = ctx.enter_context(tc.tile_pool(name="inp", bufs=1))
+        wpool = ctx.enter_context(tc.tile_pool(name="wpool", bufs=1))
+        zpool = ctx.enter_context(tc.tile_pool(name="zpool", bufs=4))
+        work = ctx.enter_context(tc.tile_pool(name="work", bufs=2))
+        psum = ctx.enter_context(tc.psum_pool(name="psum", bufs=1))
+        if MANUAL:
+            ctx.enter_context(tc.manual_schedule())
+
+        xv = x.rearrange("(p t) k -> p (t k)", t=NT)
+        sv = state.rearrange("(p t) k -> p (t k)", t=NT)
+        cv = cell.rearrange("(p t) k -> p (t k)", t=NT)
+        o0v = out_0.rearrange("(p t) h -> p (t h)", t=NT)
+        o1v = out_1.rearrange("(p t) h -> p (t h)", t=NT)
+        wiv = W_in.rearrange("n h k -> (n h) k").rearrange("(a p) k -> p a k", p=P)
+        whv = W_h.rearrange("n h k -> (n h) k").rearrange("(a p) k -> p a k", p=P)
+
+        zs, cs = {}, {}
+        wz = {}
+
+        def load_z(ci):
+            t0, n = XCH[ci]
+            zs[ci] = inp.tile([P, n * (I + H)], BF16, name="z%d" % ci)
+            rows = zs[ci][:].rearrange("p (t k) -> p t k", t=n)
+            nc.sync.dma_start(out=rows[:, :, 0:I],
+                              in_=xv[:, t0 * I:(t0 + n) * I].rearrange("p (t k) -> p t k", t=n))
+            nc.sync.dma_start(out=rows[:, :, I:I + H],
+                              in_=sv[:, t0 * H:(t0 + n) * H].rearrange("p (t k) -> p t k", t=n))
+
+        def load_c(ci):
+            t0, n = XCH[ci]
+            cs[ci] = inp.tile([P, n * H], BF16, name="c%d" % ci)
+            nc.sync.dma_start(out=cs[ci][:], in_=cv[:, t0 * H:(t0 + n) * H])
+
+        def load_w(n):
+            wz[n] = wpool.tile([P, 2 * (I + H)], BF16, name="wz%d" % n)
+            rows = wz[n][:].rearrange("p (a k) -> p a k", a=2)
+            nc.sync.dma_start(out=rows[:, :, 0:I], in_=wiv[:, 2 * n:2 * n + 2, :])
+            nc.sync.dma_start(out=rows[:, :, I:I + H], in_=whv[:, 2 * n:2 * n + 2, :])
+
+        loads = []
+        for ci, (t0, n) in enumerate(XCH):
+            loads.append((t0 // 2 - LEAD_T, 0, load_z, ci))
+            loads.append((t0 // 2, 1, load_c, ci))
+        loads = [e for e in sorted(loads, key=lambda e: (e[0], e[1])) if e[3] > 0]
+        done = [0]
+
+        def emit_loads(s):
+            while done[0] < len(loads) and loads[done[0]][0] - MARGIN <= s:
+                e = loads[done[0]]
+                done[0] += 1
+                e[2](e[3])
+
+        load_w(FG)
+        load_w(UG)
+        load_z(0)
+        load_w(IG)
+        load_w(OG)
+        load_c(0)
+        emit_loads(-LEAD_T)
+
+        ident_f = const.tile([P, P], F32, name="ident_f")
+        make_identity(nc, ident_f[:])
+        warm = const.tile([P, 8], F32, name="warm")
+        nc.vector.memset(warm[:], 0.0)
+        nc.scalar.activation(out=warm[:], in_=warm[:], func=ACTF.Sigmoid)
+
+        TB, GRP, ZC, ZS, BK = {}, {}, {}, {}, {}
+        SG = {}
+        US, T4 = {}, {}
+        wc, ws = {}, {}
+        copied = set()
+        quantised = set()
+
+        def ok(k):
+            return 0 <= k < NP
+
+        def tr(k):
+            TB[k] = psum.tile([P, 512], F32, name="tb", tag="T", bufs=2)
+            for u in range(2):
+                for t in range(2):
+                    ci, off = chunk_of(2 * k + t)
+                    v = zs[ci][:].bitcast(F32)
+                    nc.tensor.transpose(TB[k][:, u * 256 + t * P:u * 256 + (t + 1) * P],
+                                        v[:, off * 256 + u:(off + 1) * 256:2], ident_f[:])
+
+        def interleave(eng_copy, dst_f32, bank):
+            eng_copy(out=dst_f32.rearrange("p (c u) -> p c u", u=2),
+                     in_=bank[:].rearrange("p (u c) -> p c u", u=2))
+
+        def ev(k):
+            g, pos = group_of(k)
+            if pos == 0:
+                GRP[g] = zpool.tile([P, 2048], BF16, name="grp", tag="grp", align_bytes=64)
+            interleave(nc.scalar.copy, GRP[g][:].bitcast(F32)[:, pos * 512:(pos + 1) * 512], TB[k])
+            copied.add(k)
+
+        def qz(g):
+            n = GROUPS[g][1]
+            ZC[g] = zpool.tile([P, 512], U32, name="zc", tag="zc", align_bytes=64)
+            ZS[g] = zpool.tile([P, 512], U8, name="zs", tag="zs", align_bytes=64)
+            nc.vector.quantize_mx(out=ZC[g][:, :n * 256].bitcast(FP8X4), scales=ZS[g][:, :n * 256],
+                                  in_=GRP[g][:, :n * 1024])
+            quantised.add(g)
+
+        def mx(k, n):
+            g, pos = group_of(k)
+            BK[(n, k)] = psum.tile([P, 512], F32, name="bk" + TAGS[n], tag=TAGS[n], bufs=2 if n == UG else 1)
+            for t in range(2):
+                c0 = (2 * pos + t) * P
+                nc.tensor.matmul_mx(out=BK[(n, k)][:, t * H:(t + 1) * H],
+                                    lhsT=ZC[g][:, c0:c0 + P].bitcast(FP8X4),
+                                    lhsT_scale=ZS[g][:, c0:c0 + P],
+                                    rhs=wc[n][:].bitcast(FP8X4),
+                                    rhs_scale=ws[n][:],
+                                    start=True, stop=True)
+
+        def act(k, n):
+            g, pos = group_of(k)
+            if pos == 0:
+                SG[(n, g)] = work.tile([P, 1024], F32, name="sg" + TAGS[n], tag="sg" + TAGS[n],
+                                       bufs=4 if n in (FG, OG) else 3)
+            dst = SG[(n, g)][:, pos * 512:(pos + 1) * 512]
+            if n == UG and rr(g):
+                nc.scalar.activation(out=dst, in_=BK[(n, k)][:], func=ACTF.Relu, bias=1.0, scale=-1.0)
+                if pos == GROUPS[g][1] - 1:
+                    whole = SG[(n, g)][:, :cols(g)]
+                    nc.scalar.activation(out=whole, in_=whole, func=ACTF.Relu, bias=2.0, scale=-1.0)
+            elif n == UG:
+                nc.scalar.activation(out=dst, in_=BK[(n, k)][:], func=ACTF.Relu, bias=1.0)
+            else:
+                nc.scalar.activation(out=dst, in_=BK[(n, k)][:], func=ACTF.Sigmoid)
+
+        def w_gate(n, eng_copy):
+            wb = psum.tile([P, 512], F32, name="wb", tag=TAGS[n], bufs=2 if n == UG else 1)
+            v = wz[n][:].bitcast(F32)
+            for u in range(2):
+                for r in range(2):
+                    nc.tensor.transpose(wb[:, u * 256 + r * P:u * 256 + (r + 1) * P],
+                                        v[:, r * 256 + u:(r + 1) * 256:2], ident_f[:])
+            wg = wpool.tile([P, 1024], BF16, name="wg%d" % n, align_bytes=64)
+            interleave(eng_copy, wg[:].bitcast(F32), wb)
+            wc[n] = wpool.tile([P, 256], U32, name="wc%d" % n, align_bytes=64)
+            ws[n] = wpool.tile([P, 256], U8, name="ws%d" % n, align_bytes=64)
+            nc.vector.quantize_mx(out=wc[n][:].bitcast(FP8X4), scales=ws[n][:], in_=wg[:])
+
+        def rr(g):
+            return g >= RR_FROM and (g - RR_FROM) % RR_EVERY == 0
+
+        def cols(g):
+            return GROUPS[g][1] * 512
+
+        def dram_cols(g):
+            k0, n = GROUPS[g]
+            return slice(2 * k0 * H, 2 * (k0 + n) * H)
+
+        def clip_u(g):
+            w = cols(g)
+            US[g] = work.tile([P, 1024], F32, name="us", tag="us")
+            if g < D_UNTIL:
+                for j in range(GROUPS[g][1]):
+                    nc.vector.tensor_scalar(out=US[g][:, j * 512:(j + 1) * 512], in0=BK[(UG, GROUPS[g][0] + j)][:],
+                                            scalar1=-1.0, scalar2=1.0, op0=ALU.max, op1=ALU.min)
+                return
+            nc.vector.tensor_scalar(out=US[g][:, :w], in0=SG[(UG, g)][:, :w], scalar1=2.0, scalar2=-1.0,
+                                    op0=ALU.min, op1=ALU.add)
+
+        def f_cell(g):
+            w = cols(g)
+            ci, off = chunk_of(2 * GROUPS[g][0])
+            f = SG[(FG, g)][:, :w]
+            nc.vector.tensor_tensor(out=f, in0=f, in1=cs[ci][:, off * H:off * H + w], op=ALU.mult)
+
+        def i_u(g):
+            w = cols(g)
+            if rr(g):
+                US[g] = work.tile([P, 1024], F32, name="us", tag="us")
+                nc.vector.scalar_tensor_tensor(out=US[g][:, :w], in0=SG[(UG, g)][:, :w], scalar=-1.0,
+                                               in1=SG[(IG, g)][:, :w], op0=ALU.add, op1=ALU.mult)
+                return
+            nc.vector.tensor_tensor(out=US[g][:, :w], in0=SG[(IG, g)][:, :w], in1=US[g][:, :w], op=ALU.mult)
+
+        def new_cell(g):
+            w = cols(g)
+            f = SG[(FG, g)][:, :w]
+            nc.vector.tensor_tensor(out=f, in0=f, in1=US[g][:, :w], op=ALU.add)
+            nc.sync.dma_start(out=o1v[:, dram_cols(g)], in_=f)
+
+        def clip_c(g):
+            w = cols(g)
+            T4[g] = work.tile([P, 1024], F32, name="t4", tag="t4")
+            nc.vector.tensor_scalar(out=T4[g][:, :w], in0=SG[(FG, g)][:, :w], scalar1=-1.0, scalar2=1.0,
+                                    op0=ALU.max, op1=ALU.min)
+
+        def new_state(g):
+            w = cols(g)
+            o = SG[(OG, g)][:, :w]
+            nc.vector.tensor_tensor(out=o, in0=o, in1=T4[g][:, :w], op=ALU.mult)
+            nc.sync.dma_start(out=o0v[:, dram_cols(g)], in_=o)
+
+        def ready(g):
+            k0, n = GROUPS[g]
+            return all((k0 + j) in copied for j in range(n))
+
+        w_gate(FG, nc.scalar.copy)
+        w_gate(UG, nc.scalar.copy)
+        tr(0)
+        ev(0)
+        tr(1)
+        ev(1)
+        qz(0)
+        w_gate(IG, nc.vector.tensor_copy)
+        qz(1)
+        w_gate(OG, nc.vector.tensor_copy)
+        nxt = [2]
+        order = (FG, UG, IG, OG)
+        for s in range(-LEAD_S, NP):
+            emit_loads(s)
+            if ok(s) and group_of(s)[1] == GROUPS[group_of(s)[0]][1] - 1:
+                g = group_of(s)[0]
+                f_cell(g)
+                if g > 0:
+                    clip_c(g - 1)
+                if not rr(g):
+                    clip_u(g)
+                else:
+                    i_u(g)
+                if g > 0:
+                    new_state(g - 1)
+                if not rr(g):
+                    i_u(g)
+                if g + 2 < NG and (g + 2) not in quantised and ready(g + 2):
+                    qz(g + 2)
+                new_cell(g)
+            k = s + LEAD_S
+            if ok(k):
+                if group_of(k)[0] not in quantised:
+                    qz(group_of(k)[0])
+                for n in order:
+                    mx(k, n)
+            first = nxt[0]
+            while nxt[0] <= min(s + LEAD_T, NP - 1) and nxt[0] - first < 2:
+                tr(nxt[0])
+                nxt[0] += 1
+            if ok(k):
+                for n in order:
+                    if n != UG or group_of(k)[0] >= D_UNTIL:
+                        act(k, n)
+            for j in range(first, nxt[0]):
+                ev(j)
+        clip_c(NG - 1)
+        new_state(NG - 1)

@@ -156,7 +156,7 @@ def tile_lstmhardcell_t_kernel(tc, x, state, cell, W_in, W_h, out_0, out_1):
 
         def mx(k, n):
             g, pos = group_of(k)
-            BK[(n, k)] = psum.tile([P, 512], F32, name="bk" + TAGS[n], tag=TAGS[n], bufs=2 if n == UG else 1)
+            BK[(n, k)] = psum.tile([P, 512], F32, name="bk", tag="G", bufs=6)
             for t in range(2):
                 c0 = (2 * pos + t) * P
                 nc.tensor.matmul_mx(out=BK[(n, k)][:, t * H:(t + 1) * H],
@@ -183,7 +183,7 @@ def tile_lstmhardcell_t_kernel(tc, x, state, cell, W_in, W_h, out_0, out_1):
                 nc.scalar.activation(out=dst, in_=BK[(n, k)][:], func=ACTF.Sigmoid)
 
         def w_gate(n, eng_copy):
-            wb = psum.tile([P, 512], F32, name="wb", tag=TAGS[n], bufs=2 if n == UG else 1)
+            wb = psum.tile([P, 512], F32, name="wb", tag="G", bufs=6)
             v = wz[n][:].bitcast(F32)
             for u in range(2):
                 for r in range(2):

@@ -17,17 +17,17 @@ NT = B // P
 NP = NT // 2
 FLOPS = 2 * B * (I + H) * G * H
 
-MANUAL = False
+WARM_UPS = 5
 LEAD_T = 6
 LEAD_S = 2
 MARGIN = 8
-RR_FROM = 6
-RR_EVERY = 3
+RR_FROM = 10
+RR_EVERY = 2
 D_UNTIL = 4
 
 GROUPS = [(k, 1) for k in range(4)] + [(k, 2) for k in range(4, NP - 2, 2)] + [(NP - 2, 1), (NP - 1, 1)]
 NG = len(GROUPS)
-XCH = [(0, 4), (4, 4)] + [(t, 8) for t in range(8, NT, 8)]
+XCH = [(0, 2), (2, 2), (4, 4)] + [(t, 8) for t in range(8, NT, 8)]
 FG, IG, OG, UG = 0, 1, 2, 3
 TAGS = ["F", "I", "O", "U"]
 
@@ -55,8 +55,6 @@ def tile_lstmhardcell_t_kernel(tc, x, state, cell, W_in, W_h, out_0, out_1):
         zpool = ctx.enter_context(tc.tile_pool(name="zpool", bufs=4))
         work = ctx.enter_context(tc.tile_pool(name="work", bufs=2))
         psum = ctx.enter_context(tc.psum_pool(name="psum", bufs=1))
-        if MANUAL:
-            ctx.enter_context(tc.manual_schedule())
 
         xv = x.rearrange("(p t) k -> p (t k)", t=NT)
         sv = state.rearrange("(p t) k -> p (t k)", t=NT)
@@ -103,15 +101,20 @@ def tile_lstmhardcell_t_kernel(tc, x, state, cell, W_in, W_h, out_0, out_1):
                 e[2](e[3])
 
         load_w(FG)
-        load_w(UG)
         load_z(0)
+        load_w(UG)
+        load_c(0)
         load_w(IG)
         load_w(OG)
-        load_c(0)
         emit_loads(-LEAD_T)
 
         ident_f = const.tile([P, P], F32, name="ident_f")
         make_identity(nc, ident_f[:])
+        zeros = const.tile([P, 512], BF16, name="zeros")
+        nc.vector.memset(zeros[:], 0.0)
+        warm_up = psum.tile([P, 512], F32, name="warm_up", tag="G", bufs=6)
+        for j in range(WARM_UPS):
+            nc.tensor.matmul(warm_up[:], lhsT=zeros[:, :P], rhs=zeros[:], start=True, stop=True)
         warm = const.tile([P, 8], F32, name="warm")
         nc.vector.memset(warm[:], 0.0)
         nc.scalar.activation(out=warm[:], in_=warm[:], func=ACTF.Sigmoid)
@@ -254,15 +257,15 @@ def tile_lstmhardcell_t_kernel(tc, x, state, cell, W_in, W_h, out_0, out_1):
             return all((k0 + j) in copied for j in range(n))
 
         w_gate(FG, nc.scalar.copy)
-        w_gate(UG, nc.scalar.copy)
         tr(0)
         ev(0)
+        qz(0)
+        w_gate(UG, nc.scalar.copy)
+        w_gate(IG, nc.vector.tensor_copy)
+        w_gate(OG, nc.vector.tensor_copy)
         tr(1)
         ev(1)
-        qz(0)
-        w_gate(IG, nc.vector.tensor_copy)
         qz(1)
-        w_gate(OG, nc.vector.tensor_copy)
         nxt = [2]
         order = (FG, UG, IG, OG)
         for s in range(-LEAD_S, NP):
@@ -280,8 +283,9 @@ def tile_lstmhardcell_t_kernel(tc, x, state, cell, W_in, W_h, out_0, out_1):
                     new_state(g - 1)
                 if not rr(g):
                     i_u(g)
-                if g + 2 < NG and (g + 2) not in quantised and ready(g + 2):
-                    qz(g + 2)
+                for a in (2, 3):
+                    if g + a < NG and (g + a) not in quantised and ready(g + a) and (a == 2 or g + a == NG - 1):
+                        qz(g + a)
                 new_cell(g)
             k = s + LEAD_S
             if ok(k):

@@ -21,8 +21,8 @@ WARM_UPS = 5
 LEAD_T = 6
 LEAD_S = 2
 MARGIN = 8
-RR_FROM = 10
-RR_EVERY = 2
+RR_FROM = 12
+PE_GROUPS = range(5, 16, 2)
 D_UNTIL = 4
 
 GROUPS = [(k, 1) for k in range(4)] + [(k, 2) for k in range(4, NP - 2, 2)] + [(NP - 2, 1), (NP - 1, 1)]
@@ -110,9 +110,11 @@ def tile_lstmhardcell_t_kernel(tc, x, state, cell, W_in, W_h, out_0, out_1):
 
         ident_f = const.tile([P, P], F32, name="ident_f")
         make_identity(nc, ident_f[:])
+        minus_ident = const.tile([P, P], F32, name="minus_ident")
+        nc.vector.tensor_scalar(out=minus_ident[:], in0=ident_f[:], scalar1=-1.0, scalar2=None, op0=ALU.mult)
         zeros = const.tile([P, 512], BF16, name="zeros")
         nc.vector.memset(zeros[:], 0.0)
-        warm_up = psum.tile([P, 512], F32, name="warm_up", tag="G", bufs=6)
+        warm_up = psum.tile([P, 512], F32, name="warm_up", tag="G", bufs=5)
         for j in range(WARM_UPS):
             nc.tensor.matmul(warm_up[:], lhsT=zeros[:, :P], rhs=zeros[:], start=True, stop=True)
         warm = const.tile([P, 8], F32, name="warm")
@@ -121,7 +123,7 @@ def tile_lstmhardcell_t_kernel(tc, x, state, cell, W_in, W_h, out_0, out_1):
 
         TB, GRP, ZC, ZS, BK = {}, {}, {}, {}, {}
         SG = {}
-        US, T4 = {}, {}
+        US, T4, NB = {}, {}, {}
         wc, ws = {}, {}
         copied = set()
         quantised = set()
@@ -159,7 +161,7 @@ def tile_lstmhardcell_t_kernel(tc, x, state, cell, W_in, W_h, out_0, out_1):
 
         def mx(k, n):
             g, pos = group_of(k)
-            BK[(n, k)] = psum.tile([P, 512], F32, name="bk", tag="G", bufs=6)
+            BK[(n, k)] = psum.tile([P, 512], F32, name="bk", tag="G", bufs=5)
             for t in range(2):
                 c0 = (2 * pos + t) * P
                 nc.tensor.matmul_mx(out=BK[(n, k)][:, t * H:(t + 1) * H],
@@ -173,7 +175,7 @@ def tile_lstmhardcell_t_kernel(tc, x, state, cell, W_in, W_h, out_0, out_1):
             g, pos = group_of(k)
             if pos == 0:
                 SG[(n, g)] = work.tile([P, 1024], F32, name="sg" + TAGS[n], tag="sg" + TAGS[n],
-                                       bufs=4 if n in (FG, OG) else 3)
+                                       bufs=5 if n in (FG, OG) else 4)
             dst = SG[(n, g)][:, pos * 512:(pos + 1) * 512]
             if n == UG and rr(g):
                 nc.scalar.activation(out=dst, in_=BK[(n, k)][:], func=ACTF.Relu, bias=1.0, scale=-1.0)
@@ -186,7 +188,7 @@ def tile_lstmhardcell_t_kernel(tc, x, state, cell, W_in, W_h, out_0, out_1):
                 nc.scalar.activation(out=dst, in_=BK[(n, k)][:], func=ACTF.Sigmoid)
 
         def w_gate(n, eng_copy):
-            wb = psum.tile([P, 512], F32, name="wb", tag="G", bufs=6)
+            wb = psum.tile([P, 512], F32, name="wb", tag="G", bufs=5)
             v = wz[n][:].bitcast(F32)
             for u in range(2):
                 for r in range(2):
@@ -199,7 +201,7 @@ def tile_lstmhardcell_t_kernel(tc, x, state, cell, W_in, W_h, out_0, out_1):
             nc.vector.quantize_mx(out=wc[n][:].bitcast(FP8X4), scales=ws[n][:], in_=wg[:])
 
         def rr(g):
-            return g >= RR_FROM and (g - RR_FROM) % RR_EVERY == 0
+            return g >= RR_FROM and g not in PE_GROUPS
 
         def cols(g):
             return GROUPS[g][1] * 512
@@ -216,7 +218,8 @@ def tile_lstmhardcell_t_kernel(tc, x, state, cell, W_in, W_h, out_0, out_1):
                     nc.vector.tensor_scalar(out=US[g][:, j * 512:(j + 1) * 512], in0=BK[(UG, GROUPS[g][0] + j)][:],
                                             scalar1=-1.0, scalar2=1.0, op0=ALU.max, op1=ALU.min)
                 return
-            nc.vector.tensor_scalar(out=US[g][:, :w], in0=SG[(UG, g)][:, :w], scalar1=2.0, scalar2=-1.0,
+            a = 512 if g in PE_GROUPS else 0
+            nc.vector.tensor_scalar(out=US[g][:, a:w], in0=SG[(UG, g)][:, a:w], scalar1=2.0, scalar2=-1.0,
                                     op0=ALU.min, op1=ALU.add)
 
         def f_cell(g):
@@ -232,13 +235,37 @@ def tile_lstmhardcell_t_kernel(tc, x, state, cell, W_in, W_h, out_0, out_1):
                 nc.vector.scalar_tensor_tensor(out=US[g][:, :w], in0=SG[(UG, g)][:, :w], scalar=-1.0,
                                                in1=SG[(IG, g)][:, :w], op0=ALU.add, op1=ALU.mult)
                 return
-            nc.vector.tensor_tensor(out=US[g][:, :w], in0=SG[(IG, g)][:, :w], in1=US[g][:, :w], op=ALU.mult)
+            a = 512 if g in PE_GROUPS else 0
+            nc.vector.tensor_tensor(out=US[g][:, a:w], in0=SG[(IG, g)][:, a:w], in1=US[g][:, a:w], op=ALU.mult)
 
         def new_cell(g):
             w = cols(g)
-            f = SG[(FG, g)][:, :w]
-            nc.vector.tensor_tensor(out=f, in0=f, in1=US[g][:, :w], op=ALU.add)
-            nc.sync.dma_start(out=o1v[:, dram_cols(g)], in_=f)
+            a = 512 if g in PE_GROUPS else 0
+            f = SG[(FG, g)][:, a:w]
+            nc.vector.tensor_tensor(out=f, in0=f, in1=US[g][:, a:w], op=ALU.add)
+            if g not in PE_GROUPS:
+                nc.sync.dma_start(out=o1v[:, dram_cols(g)], in_=f)
+
+        def i_u1(g):
+            part = slice(0, 512)
+            u = SG[(UG, g)][:, part]
+            nc.vector.scalar_tensor_tensor(out=u, in0=u, scalar=2.0, in1=SG[(IG, g)][:, part],
+                                           op0=ALU.min, op1=ALU.mult)
+
+        def pe_add(g, stage):
+            part = slice(0, 512)
+            if stage == 0:
+                NB[g] = psum.tile([P, 512], F32, name="nb", tag="N", bufs=1)
+                nc.tensor.matmul(NB[g][:], lhsT=minus_ident[:], rhs=SG[(IG, g)][:, part], start=True, stop=False)
+                return
+            if stage == 1:
+                nc.tensor.matmul(NB[g][:], lhsT=ident_f[:], rhs=SG[(FG, g)][:, part], start=False, stop=False)
+                return
+            if stage == 2:
+                nc.tensor.matmul(NB[g][:], lhsT=ident_f[:], rhs=SG[(UG, g)][:, part], start=False, stop=True)
+                return
+            nc.scalar.copy(out=SG[(FG, g)][:, part], in_=NB[g][:])
+            nc.sync.dma_start(out=o1v[:, dram_cols(g)], in_=SG[(FG, g)][:, :cols(g)])
 
         def clip_c(g):
             w = cols(g)
@@ -267,31 +294,40 @@ def tile_lstmhardcell_t_kernel(tc, x, state, cell, W_in, W_h, out_0, out_1):
         ev(1)
         qz(1)
         nxt = [2]
+        pending, adds = [], []
         order = (FG, UG, IG, OG)
         for s in range(-LEAD_S, NP):
             emit_loads(s)
             if ok(s) and group_of(s)[1] == GROUPS[group_of(s)[0]][1] - 1:
                 g = group_of(s)[0]
                 f_cell(g)
-                if g > 0:
-                    clip_c(g - 1)
+                due = [d for d in pending if d + (2 if d in PE_GROUPS else 1) <= g]
+                for d in due:
+                    clip_c(d)
+                    pending.remove(d)
+                if g in PE_GROUPS:
+                    i_u1(g)
                 if not rr(g):
                     clip_u(g)
-                else:
-                    i_u(g)
-                if g > 0:
-                    new_state(g - 1)
-                if not rr(g):
-                    i_u(g)
+                for d in due:
+                    new_state(d)
+                i_u(g)
                 for a in (2, 3):
                     if g + a < NG and (g + a) not in quantised and ready(g + a) and (a == 2 or g + a == NG - 1):
                         qz(g + a)
+                if g in PE_GROUPS:
+                    adds = [(g, 0), (g, 1), (g, 2), (g, 3)]
                 new_cell(g)
+                pending.append(g)
             k = s + LEAD_S
             if ok(k):
                 if group_of(k)[0] not in quantised:
                     qz(group_of(k)[0])
-                for n in order:
+                for n in order[:2]:
+                    mx(k, n)
+                if adds:
+                    pe_add(*adds.pop(0))
+                for n in order[2:]:
                     mx(k, n)
             first = nxt[0]
             while nxt[0] <= min(s + LEAD_T, NP - 1) and nxt[0] - first < 2:
@@ -303,5 +339,9 @@ def tile_lstmhardcell_t_kernel(tc, x, state, cell, W_in, W_h, out_0, out_1):
                         act(k, n)
             for j in range(first, nxt[0]):
                 ev(j)
-        clip_c(NG - 1)
-        new_state(NG - 1)
+            if adds:
+                pe_add(*adds.pop(0))
+        for d in pending:
+            clip_c(d)
+        for d in pending:
+            new_state(d)

@@ -17,15 +17,15 @@ NT = B // P
 NP = NT // 2
 FLOPS = 2 * B * (I + H) * G * H
 
-WARM_UPS = 5
+WARM_UPS = 3
 LEAD_T = 6
 LEAD_S = 2
 MARGIN = 8
-RR_FROM = 12
-PE_GROUPS = range(5, 16, 2)
+RR_FROM = 16
+PE_GROUPS = range(5, 18, 2)
 D_UNTIL = 4
 
-GROUPS = [(k, 1) for k in range(4)] + [(k, 2) for k in range(4, NP - 2, 2)] + [(NP - 2, 1), (NP - 1, 1)]
+GROUPS = [(k, 1) for k in range(4)] + [(k, 2) for k in range(4, NP - 4, 2)] + [(k, 1) for k in range(NP - 4, NP)]
 NG = len(GROUPS)
 XCH = [(0, 2), (2, 2), (4, 4)] + [(t, 8) for t in range(8, NT, 8)]
 FG, IG, OG, UG = 0, 1, 2, 3
@@ -210,6 +210,10 @@ def tile_lstmhardcell_t_kernel(tc, x, state, cell, W_in, W_h, out_0, out_1):
             k0, n = GROUPS[g]
             return slice(2 * k0 * H, 2 * (k0 + n) * H)
 
+        def parts(a, b, g):
+            m = (a + b) // 2
+            return [slice(a, m), slice(m, b)] if g == NG - 1 else [slice(a, b)]
+
         def clip_u(g):
             w = cols(g)
             US[g] = work.tile([P, 1024], F32, name="us", tag="us")
@@ -219,6 +223,8 @@ def tile_lstmhardcell_t_kernel(tc, x, state, cell, W_in, W_h, out_0, out_1):
                                             scalar1=-1.0, scalar2=1.0, op0=ALU.max, op1=ALU.min)
                 return
             a = 512 if g in PE_GROUPS else 0
+            if a == w:
+                return
             nc.vector.tensor_scalar(out=US[g][:, a:w], in0=SG[(UG, g)][:, a:w], scalar1=2.0, scalar2=-1.0,
                                     op0=ALU.min, op1=ALU.add)
 
@@ -236,15 +242,20 @@ def tile_lstmhardcell_t_kernel(tc, x, state, cell, W_in, W_h, out_0, out_1):
                                                in1=SG[(IG, g)][:, :w], op0=ALU.add, op1=ALU.mult)
                 return
             a = 512 if g in PE_GROUPS else 0
+            if a == w:
+                return
             nc.vector.tensor_tensor(out=US[g][:, a:w], in0=SG[(IG, g)][:, a:w], in1=US[g][:, a:w], op=ALU.mult)
 
         def new_cell(g):
             w = cols(g)
             a = 512 if g in PE_GROUPS else 0
-            f = SG[(FG, g)][:, a:w]
-            nc.vector.tensor_tensor(out=f, in0=f, in1=US[g][:, a:w], op=ALU.add)
+            if a == w:
+                return
+            for part in parts(a, w, g):
+                f = SG[(FG, g)][:, part]
+                nc.vector.tensor_tensor(out=f, in0=f, in1=US[g][:, part], op=ALU.add)
             if g not in PE_GROUPS:
-                nc.sync.dma_start(out=o1v[:, dram_cols(g)], in_=f)
+                nc.sync.dma_start(out=o1v[:, dram_cols(g)], in_=SG[(FG, g)][:, :w])
 
         def i_u1(g):
             part = slice(0, 512)
@@ -270,14 +281,17 @@ def tile_lstmhardcell_t_kernel(tc, x, state, cell, W_in, W_h, out_0, out_1):
         def clip_c(g):
             w = cols(g)
             T4[g] = work.tile([P, 1024], F32, name="t4", tag="t4")
-            nc.vector.tensor_scalar(out=T4[g][:, :w], in0=SG[(FG, g)][:, :w], scalar1=-1.0, scalar2=1.0,
-                                    op0=ALU.max, op1=ALU.min)
+            for part in parts(0, w, g):
+                nc.vector.tensor_scalar(out=T4[g][:, part], in0=SG[(FG, g)][:, part], scalar1=-1.0, scalar2=1.0,
+                                        op0=ALU.max, op1=ALU.min)
 
         def new_state(g):
             w = cols(g)
-            o = SG[(OG, g)][:, :w]
-            nc.vector.tensor_tensor(out=o, in0=o, in1=T4[g][:, :w], op=ALU.mult)
-            nc.sync.dma_start(out=o0v[:, dram_cols(g)], in_=o)
+            first = dram_cols(g).start
+            for part in parts(0, w, g):
+                o = SG[(OG, g)][:, part]
+                nc.vector.tensor_tensor(out=o, in0=o, in1=T4[g][:, part], op=ALU.mult)
+                nc.sync.dma_start(out=o0v[:, first + part.start:first + part.stop], in_=o)
 
         def ready(g):
             k0, n = GROUPS[g]
@@ -307,14 +321,17 @@ def tile_lstmhardcell_t_kernel(tc, x, state, cell, W_in, W_h, out_0, out_1):
                     pending.remove(d)
                 if g in PE_GROUPS:
                     i_u1(g)
-                if not rr(g):
+                if rr(g):
+                    i_u(g)
+                else:
                     clip_u(g)
                 for d in due:
                     new_state(d)
-                i_u(g)
-                for a in (2, 3):
-                    if g + a < NG and (g + a) not in quantised and ready(g + a) and (a == 2 or g + a == NG - 1):
-                        qz(g + a)
+                if not rr(g):
+                    i_u(g)
+                for a in range(g + 1, NG):
+                    if GROUPS[a][0] <= s + (4 if s >= D_UNTIL - 1 else 2) and a not in quantised and ready(a):
+                        qz(a)
                 if g in PE_GROUPS:
                     adds = [(g, 0), (g, 1), (g, 2), (g, 3)]
                 new_cell(g)
@@ -339,8 +356,10 @@ def tile_lstmhardcell_t_kernel(tc, x, state, cell, W_in, W_h, out_0, out_1):
                         act(k, n)
             for j in range(first, nxt[0]):
                 ev(j)
-            if adds:
+            while adds:
                 pe_add(*adds.pop(0))
+                if ok(k):
+                    break
         for d in pending:
             clip_c(d)
         for d in pending:

from contextlib import ExitStack

import concourse.mybir as mybir
from concourse.masks import make_identity

F32 = mybir.dt.float32
BF16 = mybir.dt.bfloat16
U32 = mybir.dt.uint32
U8 = mybir.dt.uint8
FP8X4 = mybir.dt.float8_e4m3fn_x4
ALU = mybir.AluOpType
ACTF = mybir.ActivationFunctionType

P = 128
B, I, H, G = 8192, 256, 256, 4
NT = B // P
NP = NT // 2
FLOPS = 2 * B * (I + H) * G * H

WARM_UPS = 3
LEAD_T = 6
LEAD_S = 2
MARGIN = 8
RR_FROM = 16
PE_GROUPS = range(5, 18, 2)
D_UNTIL = 4

GROUPS = [(k, 1) for k in range(4)] + [(k, 2) for k in range(4, NP - 4, 2)] + [(k, 1) for k in range(NP - 4, NP)]
NG = len(GROUPS)
XCH = [(0, 2), (2, 2), (4, 4)] + [(t, 8) for t in range(8, NT, 8)]
FG, IG, OG, UG = 0, 1, 2, 3
TAGS = ["F", "I", "O", "U"]


def chunk_of(t):
    for ci, (t0, n) in enumerate(XCH):
        if t0 <= t < t0 + n:
            return ci, t - t0
    raise ValueError("tile outside the table")


def group_of(k):
    for g, (k0, n) in enumerate(GROUPS):
        if k0 <= k < k0 + n:
            return g, k - k0
    raise ValueError("pair outside the table")


def tile_lstmhardcell_t_kernel(tc, x, state, cell, W_in, W_h, out_0, out_1):
    nc = tc.nc
    with ExitStack() as ctx:
        const = ctx.enter_context(tc.tile_pool(name="const", bufs=1))
        inp = ctx.enter_context(tc.tile_pool(name="inp", bufs=1))
        wpool = ctx.enter_context(tc.tile_pool(name="wpool", bufs=1))
        zpool = ctx.enter_context(tc.tile_pool(name="zpool", bufs=4))
        work = ctx.enter_context(tc.tile_pool(name="work", bufs=2))
        psum = ctx.enter_context(tc.psum_pool(name="psum", bufs=1))

        xv = x.rearrange("(p t) k -> p (t k)", t=NT)
        sv = state.rearrange("(p t) k -> p (t k)", t=NT)
        cv = cell.rearrange("(p t) k -> p (t k)", t=NT)
        o0v = out_0.rearrange("(p t) h -> p (t h)", t=NT)
        o1v = out_1.rearrange("(p t) h -> p (t h)", t=NT)
        wiv = W_in.rearrange("n h k -> (n h) k").rearrange("(a p) k -> p a k", p=P)
        whv = W_h.rearrange("n h k -> (n h) k").rearrange("(a p) k -> p a k", p=P)

        zs, cs = {}, {}
        wz = {}

        def load_z(ci):
            t0, n = XCH[ci]
            zs[ci] = inp.tile([P, n * (I + H)], BF16, name="z%d" % ci)
            rows = zs[ci][:].rearrange("p (t k) -> p t k", t=n)
            nc.sync.dma_start(out=rows[:, :, 0:I],
                              in_=xv[:, t0 * I:(t0 + n) * I].rearrange("p (t k) -> p t k", t=n))
            nc.sync.dma_start(out=rows[:, :, I:I + H],
                              in_=sv[:, t0 * H:(t0 + n) * H].rearrange("p (t k) -> p t k", t=n))

        def load_c(ci):
            t0, n = XCH[ci]
            cs[ci] = inp.tile([P, n * H], BF16, name="c%d" % ci)
            nc.sync.dma_start(out=cs[ci][:], in_=cv[:, t0 * H:(t0 + n) * H])

        def load_w(n):
            wz[n] = wpool.tile([P, 2 * (I + H)], BF16, name="wz%d" % n)
            rows = wz[n][:].rearrange("p (a k) -> p a k", a=2)
            nc.sync.dma_start(out=rows[:, :, 0:I], in_=wiv[:, 2 * n:2 * n + 2, :])
            nc.sync.dma_start(out=rows[:, :, I:I + H], in_=whv[:, 2 * n:2 * n + 2, :])

        loads = []
        for ci, (t0, n) in enumerate(XCH):
            loads.append((t0 // 2 - LEAD_T, 0, load_z, ci))
            loads.append((t0 // 2, 1, load_c, ci))
        loads = [e for e in sorted(loads, key=lambda e: (e[0], e[1])) if e[3] > 0]
        done = [0]

        def emit_loads(s):
            while done[0] < len(loads) and loads[done[0]][0] - MARGIN <= s:
                e = loads[done[0]]
                done[0] += 1
                e[2](e[3])

        load_w(FG)
        load_z(0)
        load_w(UG)
        load_c(0)
        load_w(IG)
        load_w(OG)
        emit_loads(-LEAD_T)

        ident_f = const.tile([P, P], F32, name="ident_f")
        make_identity(nc, ident_f[:])
        minus_ident = const.tile([P, P], F32, name="minus_ident")
        nc.vector.tensor_scalar(out=minus_ident[:], in0=ident_f[:], scalar1=-1.0, scalar2=None, op0=ALU.mult)
        zeros = const.tile([P, 512], BF16, name="zeros")
        nc.vector.memset(zeros[:], 0.0)
        warm_up = psum.tile([P, 512], F32, name="warm_up", tag="G", bufs=5)
        for j in range(WARM_UPS):
            nc.tensor.matmul(warm_up[:], lhsT=zeros[:, :P], rhs=zeros[:], start=True, stop=True)
        warm = const.tile([P, 8], F32, name="warm")
        nc.vector.memset(warm[:], 0.0)
        nc.scalar.activation(out=warm[:], in_=warm[:], func=ACTF.Sigmoid)

        TB, GRP, ZC, ZS, BK = {}, {}, {}, {}, {}
        SG = {}
        US, T4, NB = {}, {}, {}
        wc, ws = {}, {}
        copied = set()
        quantised = set()

        def ok(k):
            return 0 <= k < NP

        def tr(k):
            TB[k] = psum.tile([P, 512], F32, name="tb", tag="T", bufs=2)
            for u in range(2):
                for t in range(2):
                    ci, off = chunk_of(2 * k + t)
                    v = zs[ci][:].bitcast(F32)
                    nc.tensor.transpose(TB[k][:, u * 256 + t * P:u * 256 + (t + 1) * P],
                                        v[:, off * 256 + u:(off + 1) * 256:2], ident_f[:])

        def interleave(eng_copy, dst_f32, bank):
            eng_copy(out=dst_f32.rearrange("p (c u) -> p c u", u=2),
                     in_=bank[:].rearrange("p (u c) -> p c u", u=2))

        def ev(k):
            g, pos = group_of(k)
            if pos == 0:
                GRP[g] = zpool.tile([P, 2048], BF16, name="grp", tag="grp", align_bytes=64)
            interleave(nc.scalar.copy, GRP[g][:].bitcast(F32)[:, pos * 512:(pos + 1) * 512], TB[k])
            copied.add(k)

        def qz(g):
            n = GROUPS[g][1]
            ZC[g] = zpool.tile([P, 512], U32, name="zc", tag="zc", align_bytes=64)
            ZS[g] = zpool.tile([P, 512], U8, name="zs", tag="zs", align_bytes=64)
            nc.vector.quantize_mx(out=ZC[g][:, :n * 256].bitcast(FP8X4), scales=ZS[g][:, :n * 256],
                                  in_=GRP[g][:, :n * 1024])
            quantised.add(g)

        def mx(k, n):
            g, pos = group_of(k)
            BK[(n, k)] = psum.tile([P, 512], F32, name="bk", tag="G", bufs=5)
            for t in range(2):
                c0 = (2 * pos + t) * P
                nc.tensor.matmul_mx(out=BK[(n, k)][:, t * H:(t + 1) * H],
                                    lhsT=ZC[g][:, c0:c0 + P].bitcast(FP8X4),
                                    lhsT_scale=ZS[g][:, c0:c0 + P],
                                    rhs=wc[n][:].bitcast(FP8X4),
                                    rhs_scale=ws[n][:],
                                    start=True, stop=True)

        def act(k, n):
            g, pos = group_of(k)
            if pos == 0:
                SG[(n, g)] = work.tile([P, 1024], F32, name="sg" + TAGS[n], tag="sg" + TAGS[n],
                                       bufs=5 if n in (FG, OG) else 4)
            dst = SG[(n, g)][:, pos * 512:(pos + 1) * 512]
            if n == UG and rr(g):
                nc.scalar.activation(out=dst, in_=BK[(n, k)][:], func=ACTF.Relu, bias=1.0, scale=-1.0)
                if pos == GROUPS[g][1] - 1:
                    whole = SG[(n, g)][:, :cols(g)]
                    nc.scalar.activation(out=whole, in_=whole, func=ACTF.Relu, bias=2.0, scale=-1.0)
            elif n == UG:
                nc.scalar.activation(out=dst, in_=BK[(n, k)][:], func=ACTF.Relu, bias=1.0)
            else:
                nc.scalar.activation(out=dst, in_=BK[(n, k)][:], func=ACTF.Sigmoid)

        def w_gate(n, eng_copy):
            wb = psum.tile([P, 512], F32, name="wb", tag="G", bufs=5)
            v = wz[n][:].bitcast(F32)
            for u in range(2):
                for r in range(2):
                    nc.tensor.transpose(wb[:, u * 256 + r * P:u * 256 + (r + 1) * P],
                                        v[:, r * 256 + u:(r + 1) * 256:2], ident_f[:])
            wg = wpool.tile([P, 1024], BF16, name="wg%d" % n, align_bytes=64)
            interleave(eng_copy, wg[:].bitcast(F32), wb)
            wc[n] = wpool.tile([P, 256], U32, name="wc%d" % n, align_bytes=64)
            ws[n] = wpool.tile([P, 256], U8, name="ws%d" % n, align_bytes=64)
            nc.vector.quantize_mx(out=wc[n][:].bitcast(FP8X4), scales=ws[n][:], in_=wg[:])

        def rr(g):
            return g >= RR_FROM and g not in PE_GROUPS

        def cols(g):
            return GROUPS[g][1] * 512

        def dram_cols(g):
            k0, n = GROUPS[g]
            return slice(2 * k0 * H, 2 * (k0 + n) * H)

        def parts(a, b, g):
            m = (a + b) // 2
            return [slice(a, m), slice(m, b)] if g == NG - 1 else [slice(a, b)]

        def clip_u(g):
            w = cols(g)
            US[g] = work.tile([P, 1024], F32, name="us", tag="us")
            if g < D_UNTIL:
                for j in range(GROUPS[g][1]):
                    nc.vector.tensor_scalar(out=US[g][:, j * 512:(j + 1) * 512], in0=BK[(UG, GROUPS[g][0] + j)][:],
                                            scalar1=-1.0, scalar2=1.0, op0=ALU.max, op1=ALU.min)
                return
            a = 512 if g in PE_GROUPS else 0
            if a == w:
                return
            nc.vector.tensor_scalar(out=US[g][:, a:w], in0=SG[(UG, g)][:, a:w], scalar1=2.0, scalar2=-1.0,
                                    op0=ALU.min, op1=ALU.add)

        def f_cell(g):
            w = cols(g)
            ci, off = chunk_of(2 * GROUPS[g][0])
            f = SG[(FG, g)][:, :w]
            nc.vector.tensor_tensor(out=f, in0=f, in1=cs[ci][:, off * H:off * H + w], op=ALU.mult)

        def i_u(g):
            w = cols(g)
            if rr(g):
                US[g] = work.tile([P, 1024], F32, name="us", tag="us")
                nc.vector.scalar_tensor_tensor(out=US[g][:, :w], in0=SG[(UG, g)][:, :w], scalar=-1.0,
                                               in1=SG[(IG, g)][:, :w], op0=ALU.add, op1=ALU.mult)
                return
            a = 512 if g in PE_GROUPS else 0
            if a == w:
                return
            nc.vector.tensor_tensor(out=US[g][:, a:w], in0=SG[(IG, g)][:, a:w], in1=US[g][:, a:w], op=ALU.mult)

        def new_cell(g):
            w = cols(g)
            a = 512 if g in PE_GROUPS else 0
            if a == w:
                return
            for part in parts(a, w, g):
                f = SG[(FG, g)][:, part]
                nc.vector.tensor_tensor(out=f, in0=f, in1=US[g][:, part], op=ALU.add)
            if g not in PE_GROUPS:
                nc.sync.dma_start(out=o1v[:, dram_cols(g)], in_=SG[(FG, g)][:, :w])

        def i_u1(g):
            part = slice(0, 512)
            u = SG[(UG, g)][:, part]
            nc.vector.scalar_tensor_tensor(out=u, in0=u, scalar=2.0, in1=SG[(IG, g)][:, part],
                                           op0=ALU.min, op1=ALU.mult)

        def pe_add(g, stage):
            part = slice(0, 512)
            if stage == 0:
                NB[g] = psum.tile([P, 512], F32, name="nb", tag="N", bufs=1)
                nc.tensor.matmul(NB[g][:], lhsT=minus_ident[:], rhs=SG[(IG, g)][:, part], start=True, stop=False)
                return
            if stage == 1:
                nc.tensor.matmul(NB[g][:], lhsT=ident_f[:], rhs=SG[(FG, g)][:, part], start=False, stop=False)
                return
            if stage == 2:
                nc.tensor.matmul(NB[g][:], lhsT=ident_f[:], rhs=SG[(UG, g)][:, part], start=False, stop=True)
                return
            nc.scalar.copy(out=SG[(FG, g)][:, part], in_=NB[g][:])
            nc.sync.dma_start(out=o1v[:, dram_cols(g)], in_=SG[(FG, g)][:, :cols(g)])

        def clip_c(g):
            w = cols(g)
            T4[g] = work.tile([P, 1024], F32, name="t4", tag="t4")
            for part in parts(0, w, g):
                nc.vector.tensor_scalar(out=T4[g][:, part], in0=SG[(FG, g)][:, part], scalar1=-1.0, scalar2=1.0,
                                        op0=ALU.max, op1=ALU.min)

        def new_state(g):
            w = cols(g)
            first = dram_cols(g).start
            for part in parts(0, w, g):
                o = SG[(OG, g)][:, part]
                nc.vector.tensor_tensor(out=o, in0=o, in1=T4[g][:, part], op=ALU.mult)
                nc.sync.dma_start(out=o0v[:, first + part.start:first + part.stop], in_=o)

        def ready(g):
            k0, n = GROUPS[g]
            return all((k0 + j) in copied for j in range(n))

        w_gate(FG, nc.scalar.copy)
        tr(0)
        ev(0)
        qz(0)
        w_gate(UG, nc.scalar.copy)
        w_gate(IG, nc.vector.tensor_copy)
        w_gate(OG, nc.vector.tensor_copy)
        tr(1)
        ev(1)
        qz(1)
        nxt = [2]
        pending, adds = [], []
        order = (FG, UG, IG, OG)
        for s in range(-LEAD_S, NP):
            emit_loads(s)
            if ok(s) and group_of(s)[1] == GROUPS[group_of(s)[0]][1] - 1:
                g = group_of(s)[0]
                f_cell(g)
                due = [d for d in pending if d + (2 if d in PE_GROUPS else 1) <= g]
                for d in due:
                    clip_c(d)
                    pending.remove(d)
                if g in PE_GROUPS:
                    i_u1(g)
                if rr(g):
                    i_u(g)
                else:
                    clip_u(g)
                for d in due:
                    new_state(d)
                if not rr(g):
                    i_u(g)
                for a in range(g + 1, NG):
                    if GROUPS[a][0] <= s + (4 if s >= D_UNTIL - 1 else 2) and a not in quantised and ready(a):
                        qz(a)
                if g in PE_GROUPS:
                    adds = [(g, 0), (g, 1), (g, 2), (g, 3)]
                new_cell(g)
                pending.append(g)
            k = s + LEAD_S
            if ok(k):
                if group_of(k)[0] not in quantised:
                    qz(group_of(k)[0])
                for n in order[:2]:
                    mx(k, n)
                if adds:
                    pe_add(*adds.pop(0))
                for n in order[2:]:
                    mx(k, n)
            first = nxt[0]
            while nxt[0] <= min(s + LEAD_T, NP - 1) and nxt[0] - first < 2:
                tr(nxt[0])
                nxt[0] += 1
            if ok(k):
                for n in order:
                    if n != UG or group_of(k)[0] >= D_UNTIL:
                        act(k, n)
            for j in range(first, nxt[0]):
                ev(j)
            while adds:
                pe_add(*adds.pop(0))
                if ok(k):
                    break
        for d in pending:
            clip_c(d)
        for d in pending:
            new_state(d)
